import numpy as np
import ml_dtypes


def mxq(x, axis, fmt="e4m3"):
    dtype, down = {"e4m3": (ml_dtypes.float8_e4m3fn, 7), "e5m2": (ml_dtypes.float8_e5m2, 14)}[fmt]
    v = np.moveaxis(np.asarray(x, np.float32).astype(ml_dtypes.bfloat16).astype(np.float64), axis, -1)
    blocks = v.reshape(v.shape[:-1] + (-1, 32))
    amax = np.abs(blocks).max(-1, keepdims=True)
    byte = np.maximum(np.where(amax > 0, np.frexp(amax)[1] - 1 + 127, 0) - down, 1)
    scale = np.exp2(byte - 127.0)
    codes = (blocks / scale).astype(np.float32).astype(dtype).astype(np.float64)
    return np.moveaxis((codes * scale).reshape(v.shape), -1, axis)


WIDE = False


def mx_kscale(k):
    if not WIDE:
        return np.ones(k)
    levels = np.array([10, -10, 5, -5, 0])
    if k % 512:
        return np.exp2(np.random.permutation(np.resize(levels, k // 32))).repeat(32)
    a = np.empty((k // 512, 16))
    for p in range(k // 512):
        a[p, :8] = np.random.permutation(np.resize(levels, 8))
        for g in range(8):
            far = levels[np.abs(levels - a[p, g]) >= 10]
            a[p, g + 8] = far[np.random.randint(len(far))]
    return np.exp2(a.ravel()).repeat(32)


BF16 = ml_dtypes.bfloat16


def bf(x):
    return np.asarray(x, np.float32).astype(BF16)


def f64(x):
    return np.asarray(x).astype(np.float64)


NF, GH, GW, NH, HD, ML = 4, 16, 16, 12, 128, 1024
S = NF * GH * GW
DIM = NH * HD
C = HD // 2
CB = C // 3
BANDS = (C - 2 * CB, CB, CB)
EPS = 1e-6
THETA = 10000.0


def rope_tables():
    pos = np.arange(ML, dtype=np.float64)
    ang = np.concatenate([np.outer(pos, 1.0 / THETA ** (np.arange(bd, dtype=np.float64) / bd)) for bd in BANDS], axis=1)
    ang = ang + np.random.uniform(0.0, 2.0 * np.pi, C)
    return np.cos(ang), np.sin(ang)


def draw0():
    s = mx_kscale(DIM)
    fc, fs = rope_tables()
    return {
        "x": bf(np.random.standard_normal((S, DIM)) * s),
        "Wq": bf(np.random.standard_normal((DIM, DIM)) / np.sqrt(DIM) / s),
        "bq": bf(np.random.standard_normal(DIM) * 0.2),
        "Wk": bf(np.random.standard_normal((DIM, DIM)) / np.sqrt(DIM) / s),
        "bk": bf(np.random.standard_normal(DIM) * 0.2),
        "gq": bf(1.0 + 0.1 * np.random.standard_normal(DIM)),
        "gk": bf(1.0 + 0.1 * np.random.standard_normal(DIM)),
        "freqs_cos": bf(fc),
        "freqs_sin": bf(fs),
    }


def rmsnorm(t, g):
    return t / np.sqrt(np.mean(t * t, axis=-1, keepdims=True) + EPS) * g


def grid_freqs(tab):
    o1, o2 = BANDS[0], BANDS[0] + BANDS[1]
    t = np.broadcast_to(tab[:NF, None, None, :o1], (NF, GH, GW, BANDS[0]))
    hh = np.broadcast_to(tab[None, :GH, None, o1:o2], (NF, GH, GW, BANDS[1]))
    ww = np.broadcast_to(tab[None, None, :GW, o2:C], (NF, GH, GW, BANDS[2]))
    return np.concatenate([t, hh, ww], axis=-1).reshape(S, C)[:, None, :]


def rope_apply(t, fc, fs):
    tr = t.reshape(S, NH, C, 2)
    a, b = tr[..., 0], tr[..., 1]
    return np.stack([a * fc - b * fs, a * fs + b * fc], axis=-1).reshape(S, NH, HD)


def core(x, Wq, bq, Wk, bk, gq, gk, freqs_cos, freqs_sin):
    xq = mxq(f64(x), 1, "e4m3")
    q = rmsnorm((xq @ mxq(f64(Wq), 1, "e4m3").T) + f64(bq), f64(gq))
    k = rmsnorm((xq @ mxq(f64(Wk), 1, "e4m3").T) + f64(bk), f64(gk))
    fc = grid_freqs(f64(freqs_cos))
    fs = grid_freqs(f64(freqs_sin))
    return rope_apply(q, fc, fs), rope_apply(k, fc, fs)


def e4m3fn_bytes(y):
    return np.clip(np.asarray(y, np.float64), -448.0, 448.0).astype(np.float32).astype(ml_dtypes.float8_e4m3fn).view(np.uint8)


def e4m3fn_values(b):
    return np.asarray(b, np.uint8).view(ml_dtypes.float8_e4m3fn).astype(np.float64)


def setup_inputs():
    d = draw0()
    x0 = np.asarray(d['Wq']).astype(np.float64)
    s = (np.max(np.abs(x0), axis=(0,), keepdims=True) / 448.0).astype(np.float32)
    out = {}
    for k, v in d.items():
        if k == 'Wq':
            out['Wq_bytes'] = e4m3fn_bytes(x0 / s.astype(np.float64))
            out['Wq_scale'] = s
        else:
            out[k] = v
    return out


def reference(x, Wq_bytes, Wq_scale, bq, Wk, bk, gq, gk, freqs_cos, freqs_sin):
    return core(x, e4m3fn_values(Wq_bytes) * Wq_scale.astype(np.float64), bq, Wk, bk, gq, gk, freqs_cos, freqs_sin)

@@ -1,0 +1,498 @@
+from contextlib import ExitStack
+
+import concourse.mybir as mybir
+from concourse.masks import make_identity
+
+F32 = mybir.dt.float32
+BF16 = mybir.dt.bfloat16
+U32 = mybir.dt.uint32
+U8 = mybir.dt.uint8
+FP8 = mybir.dt.float8_e4m3fn
+FP8X4 = mybir.dt.float8_e4m3fn_x4
+ALU = mybir.AluOpType
+ACT = mybir.ActivationFunctionType
+
+P = 128
+TOK = 1024
+DIM = 1536
+NH = 12
+PASSES = 3
+BLK = 256
+EPS = 1e-6
+W1 = 44
+W23 = 84
+FLOPS = 2 * TOK * DIM * 2 * DIM
+PS_BUFS = {"acc": 3, "bk": 5}
+HEAD_FILL = 1
+SLOT_FILL = 1
+TE_V_FROM = 6
+TE_V_J = ()
+EX_ENG = ("v", "s", "s")
+
+
+def tile_wanselfattention_pa_kernel(
+    tc, x, Wq_bytes, Wq_scale, bq, Wk, bk, gq, gk, freqs_cos, freqs_sin, out_0, out_1
+):
+    nc = tc.nc
+    outs = (out_0.rearrange("s h d -> s (h d)"), out_1.rearrange("s h d -> s (h d)"))
+
+    with ExitStack() as ctx:
+        const = ctx.enter_context(tc.tile_pool(name="const", bufs=1))
+        work = ctx.enter_context(tc.tile_pool(name="work", bufs=2))
+        psum = ctx.enter_context(tc.psum_pool(name="psum", bufs=3))
+
+        ctx.enter_context(tc.manual_schedule())
+
+        def ps_tile(shape, dtype, tag):
+            return psum.tile(shape, dtype, name="ps_" + tag, tag=tag, bufs=PS_BUFS[tag])
+
+        early_count = [0]
+
+        def early_tag():
+            early_count[0] += 1
+            return "acc" if early_count[0] % 8 < 3 else "bk"
+
+        def early_tags():
+            return (early_tag(), early_tag(), early_tag())
+
+        def evac(eng, out, in_):
+            if eng == "s":
+                nc.scalar.copy(out=out, in_=in_)
+            else:
+                nc.vector.tensor_copy(out=out, in_=in_)
+
+        scale_bc = const.tile([P, DIM], F32, name="scale_bc")
+        nc.scalar.dma_start(out=scale_bc[:], in_=Wq_scale.rearrange("o k -> (o k)").partition_broadcast(P))
+        vecs = const.tile([P, P], BF16, name="vecs")
+        nc.vector.memset(vecs[:], 0.0)
+        for i, vec in enumerate((bq, bk, gq, gk)):
+            nc.scalar.dma_start(out=vecs[NH * i : NH * (i + 1), :], in_=vec.rearrange("(h d) -> h d", d=P))
+        fc = const.tile([P, 2, 64], BF16, name="fc")
+        nc.vector.memset(fc[:], 0.0)
+        nc.scalar.dma_start(out=fc[0:16, 0, :], in_=freqs_cos[0:16, :])
+        nc.scalar.dma_start(out=fc[0:16, 1, :], in_=freqs_sin[0:16, :])
+
+        one = const.tile([P, 1], F32, name="one")
+        nc.vector.memset(one[:], 1.0)
+        warm = const.tile([P, 1], F32, name="warm")
+        nc.scalar.activation(out=warm[:], in_=one[:], func=ACT.Abs_reciprocal_sqrt)
+
+        ident_f = const.tile([P, P], F32, name="ident_f")
+        make_identity(nc, ident_f[:])
+        ident_b = const.tile([P, P], BF16, name="ident_b")
+        make_identity(nc, ident_b[:])
+
+        cx = const.tile([P, PASSES, TOK], U32, name="cx", align_bytes=64)
+        sx = const.tile([P, PASSES, TOK], U8, name="sx", align_bytes=64)
+        cw = []
+        sw = []
+        for pj in range(2):
+            cw_t = const.tile([P, PASSES, DIM], U32, name="cw%d" % pj, align_bytes=64)
+            sw_t = const.tile([P, PASSES, DIM], U8, name="sw%d" % pj, align_bytes=64)
+            cw.append(cw_t)
+            sw.append(sw_t)
+
+        st_rows = {}
+        st_tp = {}
+        st_gr = {}
+        SRC = {"x": (x, cx, sx), "q": (None, cw[0], sw[0]), "k": (Wk, cw[1], sw[1])}
+
+        def LD(s, a):
+            if s == "q":
+                wq_bytes = work.tile([P, 2, DIM], U8, name="wq_bytes", tag="wq_bytes", bufs=3)
+                nc.sync.dma_start(
+                    out=wq_bytes[:], in_=Wq_bytes[BLK * a : BLK * (a + 1), :].rearrange("(i p) k -> p i k", p=P)
+                )
+                st_rows[("qb", a)] = wq_bytes
+            else:
+                t = work.tile([P, 2, DIM], BF16, name="rows", tag="rows", bufs=4)
+                nc.sync.dma_start(
+                    out=t[:], in_=SRC[s][0][BLK * a : BLK * (a + 1), :].rearrange("(i p) k -> p i k", p=P)
+                )
+                st_rows[(s, a)] = t
+
+        def PRD(a, i):
+            if i == 0:
+                wq_val = work.tile([P, 2, DIM], BF16, name="wq_val", tag="wq_val", bufs=2)
+                st_rows[("q", a)] = wq_val
+            nc.vector.tensor_tensor(
+                out=st_rows[("q", a)][:, i, :], in0=st_rows[("qb", a)][:, i, :].bitcast(FP8), in1=scale_bc[:], op=ALU.mult
+            )
+
+        def TR(s, a, g, tag):
+            words = st_rows[(s, a)][:].rearrange("p i k -> p (i k)").bitcast(F32)
+            tp = ps_tile([P, 2, 2, P], F32, tag)
+            for i in range(2):
+                for u in range(2):
+                    base = i * (DIM // 2) + 256 * g + u
+                    nc.tensor.transpose(tp[:, i, u, :], words[:, base : base - u + 256 : 2], ident_f[:])
+            st_tp[(s, a, g)] = tp
+
+        def EX(s, a, g, eng):
+            gr = work.tile([P, BLK * 4], BF16, name="gr", tag="gr", bufs=6, align_bytes=64)
+            evac(
+                eng,
+                gr[:].bitcast(F32).rearrange("p (i r u) -> p i r u", i=2, u=2),
+                st_tp[(s, a, g)][:].rearrange("p i u r -> p i r u"),
+            )
+            st_gr[(s, a, g)] = gr
+
+        def QZ(s, a, g):
+            nc.vector.quantize_mx(
+                out=SRC[s][1][:, g, BLK * a : BLK * (a + 1)].bitcast(FP8X4),
+                scales=SRC[s][2][:, g, BLK * a : BLK * (a + 1)],
+                in_=st_gr[(s, a, g)][:],
+            )
+
+        LD("q", 0)
+        LD("x", 0)
+        for a in range(1, 3):
+            LD("q", a)
+        pending = []
+        clock = [0]
+
+        def defer(delay, fn):
+            pending.append((clock[0] + delay, fn))
+
+        def tick():
+            clock[0] += 1
+            due = [p for p in pending if p[0] <= clock[0]]
+            rest = [p for p in pending if p[0] > clock[0]]
+            pending.clear()
+            pending.extend(rest)
+            for p in due:
+                p[1]()
+
+
+        blks = [(0, 0), (0, 1), (0, 2), (0, 3), (1, 0), (1, 1), (1, 2), (1, 3)]
+        tts = {}
+        st_acc = {}
+        st_bk = {}
+        st_ss = {}
+        st_rstd = {}
+        st_uv = {}
+
+        def MXB(n, mp):
+            pj, blk = blks[n]
+            acc = ps_tile([P, 2, BLK], F32, "acc")
+            for mi in range(2):
+                m = 2 * mp + mi
+                for g in range(PASSES):
+                    nc.tensor.matmul_mx(
+                        out=acc[:, mi, :],
+                        lhsT=cw[pj][:, g, P * m : P * (m + 1)].bitcast(FP8X4),
+                        lhsT_scale=sw[pj][:, g, P * m : P * (m + 1)],
+                        rhs=cx[:, g, BLK * blk : BLK * (blk + 1)].bitcast(FP8X4),
+                        rhs_scale=sx[:, g, BLK * blk : BLK * (blk + 1)],
+                        start=(g == 0),
+                        stop=(g == PASSES - 1),
+                    )
+            st_acc[(n, mp)] = acc
+
+        def TE(n, mp, engs):
+            pj = blks[n][0]
+            for mi in range(2):
+                m = 2 * mp + mi
+                t = work.tile([P, BLK], F32, name="tT", tag="tT", bufs=26)
+                bias = cols[:, NH * pj + m : NH * pj + m + 1]
+                if engs[mi] == "s":
+                    nc.scalar.activation(out=t[:], in_=st_acc[(n, mp)][:, mi, :], func=ACT.Identity, bias=bias)
+                else:
+                    nc.vector.tensor_scalar(
+                        out=t[:], in0=st_acc[(n, mp)][:, mi, :], scalar1=bias, scalar2=None, op0=ALU.add
+                    )
+                tts[(n, m)] = t
+
+        def BT(s, b3):
+            bkt = ps_tile([P, 4, P], F32, "bk")
+            i = s % 2
+            for q in range(4):
+                nc.tensor.transpose(bkt[:, q, :], tts[(s // 2, 4 * b3 + q)][:, P * i : P * (i + 1)], ident_f[:])
+            st_bk[(s, b3)] = bkt
+
+        def SQ(s, b3):
+            if b3 == 0:
+                ss_t = work.tile([P, 8], F32, name="ss", tag="ss", bufs=4)
+                st_ss[s] = ss_t
+            junk = work.tile([P, 512], BF16, name="junk", tag="junk", bufs=2)
+            nc.scalar.activation(
+                out=junk[:],
+                in_=st_bk[(s, b3)][:].rearrange("p q d -> p (q d)"),
+                func=ACT.Square,
+                accum_out=st_ss[s][:, b3 : b3 + 1],
+            )
+
+        def RS(s):
+            ss_t = st_ss[s]
+            nc.scalar.activation(out=ss_t[:, 4:7], in_=ss_t[:, 0:3], func=ACT.Identity, accum_out=ss_t[:, 3:4])
+            nc.scalar.activation(
+                out=ss_t[:, 7:8], in_=ss_t[:, 3:4], func=ACT.Abs_reciprocal_sqrt, scale=1.0 / DIM, bias=EPS
+            )
+
+        def RC(s):
+            st_rstd[s] = st_ss[s][:, 7:8]
+
+        def UV(s, b3):
+            n = s // 2
+            parts = ((0, W1, tabs[("t1", n)]), (W1, W23, tabs[("t23", blks[n][0], s % 2)]))
+            for kind, tag in enumerate(("u", "v")):
+                pr_t = work.tile([P, 4, P], F32, name=tag, tag=tag, bufs=3)
+                for off, w, tab in parts:
+                    nc.vector.scalar_tensor_tensor(
+                        out=pr_t[:, :, off : off + w],
+                        in0=st_bk[(s, b3)][:, :, off : off + w],
+                        scalar=st_rstd[s],
+                        in1=tab[:, kind, 4 * b3 : 4 * (b3 + 1), :],
+                        op0=ALU.mult,
+                        op1=ALU.mult,
+                    )
+                st_uv[(s, b3, kind)] = pr_t
+
+        def MG(s, b3):
+            o_t = work.tile([P, 512], F32, name="o", tag="o", bufs=6)
+            eng = nc.vector if (s == 15 and b3 >= 2) else nc.gpsimd
+            eng.tensor_tensor(
+                out=o_t[:].rearrange("p (c e) -> p c e", e=2),
+                in0=st_uv[(s, b3, 0)][:].rearrange("p q (c e) -> p (q c) e", e=2),
+                in1=st_uv[(s, b3, 1)][:].rearrange("p q (c e) -> p (q c) e", e=2)[:, :, ::-1],
+                op=ALU.add,
+            )
+            pj, blk = blks[s // 2]
+            row0 = P * (2 * blk + s % 2)
+            nc.sync.dma_start(out=outs[pj][row0 : row0 + P, 512 * b3 : 512 * (b3 + 1)], in_=o_t[:])
+
+        def start_prep(src, a, g, tag, eng):
+            TR(src, a, g, tag)
+            defer(1, lambda: EX(src, a, g, eng))
+            defer(2, lambda: QZ(src, a, g))
+
+        def start_mx(n, mp, engs):
+            MXB(n, mp)
+            defer(1, lambda: TE(n, mp, engs))
+
+        fill = []
+        fill_tag = ["bk"]
+        fill_pos = [0]
+
+        def do_fill(count):
+            for r in range(count):
+                if fill_pos[0] < len(fill):
+                    fill[fill_pos[0]]()
+                    fill_pos[0] += 1
+
+        def x_jobs(a):
+            return [lambda g=g: start_prep("x", a, g, fill_tag[0], "s") for g in range(PASSES)]
+
+
+        sel = const.tile([P, 8, P], BF16, name="sel")
+        for f in range(4):
+            nc.vector.tensor_copy(out=sel[:, f, :], in_=ident_b[:, f : f + 1].to_broadcast([P, P]))
+        for hh in range(2):
+            nc.vector.tensor_copy(
+                out=sel[:, 4 + hh, :].rearrange("p (a b) -> p a b", b=16),
+                in_=ident_b[:, 8 * hh : 8 * hh + 8].unsqueeze(2).to_broadcast([P, 8, 16]),
+            )
+            nc.vector.tensor_copy(
+                out=sel[:, 6 + hh, :].rearrange("p (a b) -> p a b", b=16),
+                in_=ident_b[:, 0:16].unsqueeze(1).to_broadcast([P, 8, 16]),
+            )
+
+        for j in range(3):
+            tick()
+            if j < 2:
+                PRD(0, j)
+            else:
+                LD("q", 3)
+                LD("x", 1)
+            start_prep("x", 0, j, "bk", "s")
+
+        vps = ps_tile([P, P], BF16, "acc")
+        nc.tensor.transpose(vps[:], vecs[:], ident_b[:])
+        cols = const.tile([P, 48], F32, name="cols")
+        nc.vector.tensor_copy(out=cols[:], in_=vps[:, 0:48])
+
+        ff = const.tile([P, 2, 64, 2], BF16, name="ff")
+        nc.vector.tensor_copy(out=ff[:, 0, :, :], in_=fc[:, 0, :].unsqueeze(2).to_broadcast([P, 64, 2]))
+        nc.vector.tensor_copy(out=ff[:, 1, :, 0], in_=fc[:, 1, :])
+        nc.vector.tensor_scalar_mul(out=ff[:, 1, :, 1], in0=fc[:, 1, :], scalar1=-1.0)
+        ffv = ff[:].rearrange("p k c e -> p k (c e)")
+        ffm = const.tile([P, 2, 2, P], BF16, name="ffm")
+        nc.vector.memset(ffm[:], 0.0)
+        nc.vector.tensor_copy(out=ffm[:, 0, :, 44:86], in_=ffv[:, :, 44:86])
+        nc.vector.tensor_copy(out=ffm[:, 1, :, 86:128], in_=ffv[:, :, 86:128])
+
+        lsb = const.tile([P, 2, 6, P], BF16, name="lsb")
+        for kind in range(2):
+            lp = ps_tile([P, 512], F32, "bk")
+            nc.tensor.matmul(
+                out=lp[:], lhsT=ffv[:, kind, :], rhs=sel[:, 0:4, :].rearrange("p v q -> p (v q)"), start=True, stop=True
+            )
+            nc.scalar.copy(out=lsb[:, kind, 0:4, :].rearrange("p v q -> p (v q)"), in_=lp[:])
+            lq = ps_tile([P, 256], F32, "bk")
+            nc.tensor.matmul(
+                out=lq[:], lhsT=ffm[:, 0, kind, :], rhs=sel[:, 4:6, :].rearrange("p v q -> p (v q)"), start=True, stop=False
+            )
+            nc.tensor.matmul(
+                out=lq[:], lhsT=ffm[:, 1, kind, :], rhs=sel[:, 6:8, :].rearrange("p v q -> p (v q)"), start=False, stop=True
+            )
+            nc.scalar.copy(out=lsb[:, kind, 4:6, :].rearrange("p v q -> p (v q)"), in_=lq[:])
+
+        rd = {}
+
+        def make_rd(pj):
+            parts = []
+            for part, (off, w) in enumerate(((0, W1), (W1, W23))):
+                r_t = const.tile([P, NH, w], BF16, name="rd%d%d" % (pj, part))
+                nc.vector.tensor_tensor(
+                    out=r_t[:],
+                    in0=ident_b[:, off : off + w].unsqueeze(1).to_broadcast([P, NH, w]),
+                    in1=cols[:, 24 + NH * pj : 24 + NH * (pj + 1)].unsqueeze(2).to_broadcast([P, NH, w]),
+                    op=ALU.mult,
+                )
+                parts.append(r_t)
+            rd[pj] = parts
+
+        make_rd(0)
+
+        xx = const.tile([P, P], BF16, name="xx")
+        nc.vector.memset(xx[:], 0.0)
+        nc.vector.tensor_copy(out=xx[:, 0:8].rearrange("p (k f) -> p k f", k=2), in_=lsb[:, :, 0:4, 0])
+        scr = outs[1][TOK - 16 : TOK, :].rearrange("r c -> (r c)")
+        NROW = 16 * NH * W1
+
+        def row_jobs(pj):
+            r1 = const.tile([P, NH * W1], F32, name="r1_%d" % pj)
+            n = 6 * W1
+
+            def job(half):
+                flat = rd[pj][0][:].rearrange("p h d -> p (h d)")
+                tb = ps_tile([P, 512], F32, fill_tag[0])
+                nc.tensor.matmul(out=tb[:, 0:n], lhsT=xx[:], rhs=flat[:, n * half : n * (half + 1)], start=True, stop=True)
+                defer(1, lambda: nc.scalar.copy(out=r1[:, n * half : n * (half + 1)], in_=tb[:, 0:n]))
+
+            def store():
+                nc.sync.dma_start(
+                    out=scr[NROW * pj : NROW * (pj + 1)].rearrange("(r n) -> r n", n=NH * W1), in_=r1[0:16, :]
+                )
+
+            return [lambda: job(0), lambda: job(1), lambda: defer(2, store)]
+
+        def load_tab1(n):
+            pj, f = blks[n]
+            t = work.tile([P, 2, NH, W1], F32, name="tab1", tag="tab1", bufs=3)
+            rows = scr[NROW * pj : NROW * pj + 8 * NH * W1].rearrange("(k f n) -> f k n", k=2, f=4)
+            nc.sync.dma_start(out=t[:].rearrange("p k h d -> p k (h d)"), in_=rows[f].partition_broadcast(P))
+            tabs[("t1", n)] = t
+
+        tabs = {}
+
+        def table_jobs(pj, part, var, key):
+            w = (W1, W23)[part]
+            n = 6 * w
+            if part == 0:
+                dst = work.tile([P, 2, NH, W1], F32, name="tab1", tag="tab1", bufs=3)
+            else:
+                dst = const.tile([P, 2, NH, W23], F32, name="tab23_%d%d" % (pj, var))
+            tabs[key] = dst
+
+            def job(kind, half):
+                flat = rd[pj][part][:].rearrange("p h d -> p (h d)")
+                tb = ps_tile([P, 512], F32, fill_tag[0])
+                nc.tensor.matmul(
+                    out=tb[:, 0:n],
+                    lhsT=lsb[:, kind, var, :],
+                    rhs=flat[:, n * half : n * (half + 1)],
+                    start=True,
+                    stop=True,
+                )
+                defer(
+                    1,
+                    lambda: nc.scalar.copy(
+                        out=dst[:, kind, 6 * half : 6 * (half + 1), :].rearrange("p h d -> p (h d)"), in_=tb[:, 0:n]
+                    ),
+                )
+
+            return [lambda kind=kind, half=half: job(kind, half) for kind in range(2) for half in range(2)]
+        fill.extend(table_jobs(0, 1, 4, ("t23", 0, 0)))
+        fill.extend(row_jobs(0))
+        fill.extend(table_jobs(0, 1, 5, ("t23", 0, 1)))
+        fill.extend(x_jobs(1))
+        fill.extend(x_jobs(2))
+        fill.append(lambda: defer(3, lambda: load_tab1(0)))
+        fill.append(lambda: defer(3, lambda: load_tab1(1)))
+        fill.append(lambda: make_rd(1))
+        fill.extend(row_jobs(1))
+        fill.extend(x_jobs(3))
+        fill.extend(table_jobs(1, 1, 4, ("t23", 1, 0)))
+        fill.extend(table_jobs(1, 1, 5, ("t23", 1, 1)))
+
+        for k in range(1, 7):
+            for j in range(3):
+                tick()
+                if k < 6 and j < 2:
+                    PRD(k, j)
+                if j == 2 and k < 3:
+                    LD("q", k + 3)
+                    LD("x", k + 1)
+                if k >= 1:
+                    start_prep("q", k - 1, j, "bk", "s")
+                    if j == 2:
+                        defer(3, lambda a=k - 1: start_mx(0, a, ("s", "s")))
+                do_fill(HEAD_FILL)
+        for a in range(2):
+            LD("k", a)
+        fill_tag[0] = "acc"
+
+        def front(nx, j):
+            if j == 0:
+                BT(nx, 0)
+                BT(nx, 1)
+                SQ(nx, 0)
+                SQ(nx, 1)
+            elif j == 1:
+                BT(nx, 2)
+                SQ(nx, 2)
+                RS(nx)
+            else:
+                RC(nx)
+
+        tick()
+        front(0, 0)
+        start_mx(1, 0, ("s", "s"))
+        do_fill(1)
+        tick()
+        start_mx(1, 1, ("s", "s"))
+        do_fill(1)
+        tick()
+        do_fill(1)
+        tick()
+        front(0, 1)
+        start_mx(1, 2, ("s", "s"))
+        do_fill(1)
+        tick()
+        front(0, 2)
+
+        for s in range(16):
+            nb = (s + 1) // 2 + 1
+            mps = [3 * ((s + 1) % 2) + r for r in range(3)] if nb < 8 else []
+            for j in range(3):
+                tick()
+                if s + 1 < 16 and j < 2:
+                    front(s + 1, j)
+                UV(s, j)
+                MG(s, j)
+                if mps:
+                    te = ("s", "v") if (s >= TE_V_FROM and j in TE_V_J) else ("s", "s")
+                    start_mx(nb, mps[j], te)
+                if s <= 5:
+                    start_prep("k", s, j, "acc", EX_ENG[j])
+                    if j == 2 and s + 2 < 6:
+                        LD("k", s + 2)
+                if s + 1 < 16 and j == 2:
+                    front(s + 1, 2)
+                if j == 0 and s % 2 == 0 and s // 2 + 2 < 8:
+                    n2 = s // 2 + 2
+                    load_tab1(n2)
+                do_fill(SLOT_FILL)
+        for r in range(4):
+            tick()

@@ -62,7 +62,7 @@ def tile_wanselfattention_pa_kernel(
                 nc.vector.tensor_copy(out=out, in_=in_)
 
         scale_bc = const.tile([P, DIM], F32, name="scale_bc")
-        nc.scalar.dma_start(out=scale_bc[:], in_=Wq_scale.rearrange("o k -> (o k)").partition_broadcast(P))
+        nc.sync.dma_start(out=scale_bc[:], in_=Wq_scale.rearrange("o k -> (o k)").partition_broadcast(P))
         vecs = const.tile([P, P], BF16, name="vecs")
         nc.vector.memset(vecs[:], 0.0)
         for i, vec in enumerate((bq, bk, gq, gk)):

@@ -74,6 +74,10 @@ def tile_wanselfattention_pa_kernel(
 
         one = const.tile([P, 1], F32, name="one")
         nc.vector.memset(one[:], 1.0)
+        ffm = const.tile([P, 2, 2, P], BF16, name="ffm")
+        nc.vector.memset(ffm[:], 0.0)
+        xx = const.tile([P, P], BF16, name="xx")
+        nc.vector.memset(xx[:], 0.0)
         warm = const.tile([P, 1], F32, name="warm")
         nc.scalar.activation(out=warm[:], in_=one[:], func=ACT.Abs_reciprocal_sqrt)
 
@@ -309,17 +313,15 @@ def tile_wanselfattention_pa_kernel(
         vps = ps_tile([P, P], BF16, "acc")
         nc.tensor.transpose(vps[:], vecs[:], ident_b[:])
         cols = const.tile([P, 48], F32, name="cols")
-        nc.vector.tensor_copy(out=cols[:], in_=vps[:, 0:48])
+        nc.scalar.copy(out=cols[:], in_=vps[:, 0:48])
 
         ff = const.tile([P, 2, 64, 2], BF16, name="ff")
-        nc.vector.tensor_copy(out=ff[:, 0, :, :], in_=fc[:, 0, :].unsqueeze(2).to_broadcast([P, 64, 2]))
-        nc.vector.tensor_copy(out=ff[:, 1, :, 0], in_=fc[:, 1, :])
-        nc.vector.tensor_scalar_mul(out=ff[:, 1, :, 1], in0=fc[:, 1, :], scalar1=-1.0)
+        nc.scalar.copy(out=ff[:, 0, :, :], in_=fc[:, 0, :].unsqueeze(2).to_broadcast([P, 64, 2]))
+        nc.scalar.copy(out=ff[:, 1, :, 0], in_=fc[:, 1, :])
+        nc.scalar.mul(out=ff[:, 1, :, 1], in_=fc[:, 1, :], mul=-1.0)
         ffv = ff[:].rearrange("p k c e -> p k (c e)")
-        ffm = const.tile([P, 2, 2, P], BF16, name="ffm")
-        nc.vector.memset(ffm[:], 0.0)
-        nc.vector.tensor_copy(out=ffm[:, 0, :, 44:86], in_=ffv[:, :, 44:86])
-        nc.vector.tensor_copy(out=ffm[:, 1, :, 86:128], in_=ffv[:, :, 86:128])
+        nc.scalar.copy(out=ffm[:, 0, :, 44:86], in_=ffv[:, :, 44:86])
+        nc.scalar.copy(out=ffm[:, 1, :, 86:128], in_=ffv[:, :, 86:128])
 
         lsb = const.tile([P, 2, 6, P], BF16, name="lsb")
         for kind in range(2):
@@ -354,9 +356,7 @@ def tile_wanselfattention_pa_kernel(
 
         make_rd(0)
 
-        xx = const.tile([P, P], BF16, name="xx")
-        nc.vector.memset(xx[:], 0.0)
-        nc.vector.tensor_copy(out=xx[:, 0:8].rearrange("p (k f) -> p k f", k=2), in_=lsb[:, :, 0:4, 0])
+        nc.scalar.copy(out=xx[:, 0:8].rearrange("p (k f) -> p k f", k=2), in_=lsb[:, :, 0:4, 0])
         scr = outs[1][TOK - 16 : TOK, :].rearrange("r c -> (r c)")
         NROW = 16 * NH * W1
 

@@ -86,13 +86,13 @@ def tile_wanselfattention_pa_kernel(
         ident_b = const.tile([P, P], BF16, name="ident_b")
         make_identity(nc, ident_b[:])
 
-        cx = const.tile([P, PASSES, TOK], U32, name="cx", align_bytes=64)
-        sx = const.tile([P, PASSES, TOK], U8, name="sx", align_bytes=64)
+        cx = const.tile([P, TOK // BLK, PASSES, BLK], U32, name="cx", align_bytes=64)
+        sx = const.tile([P, TOK // BLK, PASSES, BLK], U8, name="sx", align_bytes=64)
         cw = []
         sw = []
         for pj in range(2):
-            cw_t = const.tile([P, PASSES, DIM], U32, name="cw%d" % pj, align_bytes=64)
-            sw_t = const.tile([P, PASSES, DIM], U8, name="sw%d" % pj, align_bytes=64)
+            cw_t = const.tile([P, DIM // BLK, PASSES, BLK], U32, name="cw%d" % pj, align_bytes=64)
+            sw_t = const.tile([P, DIM // BLK, PASSES, BLK], U8, name="sw%d" % pj, align_bytes=64)
             cw.append(cw_t)
             sw.append(sw_t)
 
@@ -133,19 +133,26 @@ def tile_wanselfattention_pa_kernel(
             st_tp[(s, a, g)] = tp
 
         def EX(s, a, g, eng):
-            gr = work.tile([P, BLK * 4], BF16, name="gr", tag="gr", bufs=6, align_bytes=64)
+            if g == 0:
+                gr01 = work.tile([P, 2, BLK * 4], BF16, name="gr01", tag="gr01", bufs=2, align_bytes=64)
+                st_gr[(s, a, 0)] = gr01
+            if g == 2:
+                gr2 = work.tile([P, 1, BLK * 4], BF16, name="gr2", tag="gr2", bufs=2, align_bytes=64)
+                st_gr[(s, a, 2)] = gr2
             evac(
                 eng,
-                gr[:].bitcast(F32).rearrange("p (i r u) -> p i r u", i=2, u=2),
+                st_gr[(s, a, 2 * (g // 2))][:, g % 2, :].bitcast(F32).rearrange("p (i r u) -> p i r u", i=2, u=2),
                 st_tp[(s, a, g)][:].rearrange("p i u r -> p i r u"),
             )
-            st_gr[(s, a, g)] = gr
 
         def QZ(s, a, g):
+            if g == 0:
+                return
+            g0 = 2 * (g // 2)
             nc.vector.quantize_mx(
-                out=SRC[s][1][:, g, BLK * a : BLK * (a + 1)].bitcast(FP8X4),
-                scales=SRC[s][2][:, g, BLK * a : BLK * (a + 1)],
-                in_=st_gr[(s, a, g)][:],
+                out=SRC[s][1][:, a, g0 : g + 1, :].rearrange("p g c -> p (g c)").bitcast(FP8X4),
+                scales=SRC[s][2][:, a, g0 : g + 1, :].rearrange("p g c -> p (g c)"),
+                in_=st_gr[(s, a, g0)][:].rearrange("p g c -> p (g c)"),
             )
 
         LD("q", 0)
@@ -184,10 +191,10 @@ def tile_wanselfattention_pa_kernel(
                 for g in range(PASSES):
                     nc.tensor.matmul_mx(
                         out=acc[:, mi, :],
-                        lhsT=cw[pj][:, g, P * m : P * (m + 1)].bitcast(FP8X4),
-                        lhsT_scale=sw[pj][:, g, P * m : P * (m + 1)],
-                        rhs=cx[:, g, BLK * blk : BLK * (blk + 1)].bitcast(FP8X4),
-                        rhs_scale=sx[:, g, BLK * blk : BLK * (blk + 1)],
+                        lhsT=cw[pj][:, mp, g, P * mi : P * (mi + 1)].bitcast(FP8X4),
+                        lhsT_scale=sw[pj][:, mp, g, P * mi : P * (mi + 1)],
+                        rhs=cx[:, blk, g, :].bitcast(FP8X4),
+                        rhs_scale=sx[:, blk, g, :],
                         start=(g == 0),
                         stop=(g == PASSES - 1),
                     )

@@ -295,16 +295,14 @@ def tile_wanselfattention_pa_kernel(
             return [lambda g=g: start_prep("x", a, g, fill_tag[0], "s") for g in range(PASSES)]
 
 
-        sel = const.tile([P, 8, P], BF16, name="sel")
-        for f in range(4):
-            nc.vector.tensor_copy(out=sel[:, f, :], in_=ident_b[:, f : f + 1].to_broadcast([P, P]))
+        sel = const.tile([P, 4, P], BF16, name="sel")
         for hh in range(2):
             nc.vector.tensor_copy(
-                out=sel[:, 4 + hh, :].rearrange("p (a b) -> p a b", b=16),
+                out=sel[:, hh, :].rearrange("p (a b) -> p a b", b=16),
                 in_=ident_b[:, 8 * hh : 8 * hh + 8].unsqueeze(2).to_broadcast([P, 8, 16]),
             )
             nc.vector.tensor_copy(
-                out=sel[:, 6 + hh, :].rearrange("p (a b) -> p a b", b=16),
+                out=sel[:, 2 + hh, :].rearrange("p (a b) -> p a b", b=16),
                 in_=ident_b[:, 0:16].unsqueeze(1).to_broadcast([P, 8, 16]),
             )
 
@@ -330,21 +328,20 @@ def tile_wanselfattention_pa_kernel(
         nc.scalar.copy(out=ffm[:, 0, :, 44:86], in_=ffv[:, :, 44:86])
         nc.scalar.copy(out=ffm[:, 1, :, 86:128], in_=ffv[:, :, 86:128])
 
-        lsb = const.tile([P, 2, 6, P], BF16, name="lsb")
+        lsb = const.tile([P, 2, 2, P], BF16, name="lsb")
+        fps = ps_tile([P, 2, 4], F32, "bk")
         for kind in range(2):
-            lp = ps_tile([P, 512], F32, "bk")
-            nc.tensor.matmul(
-                out=lp[:], lhsT=ffv[:, kind, :], rhs=sel[:, 0:4, :].rearrange("p v q -> p (v q)"), start=True, stop=True
-            )
-            nc.scalar.copy(out=lsb[:, kind, 0:4, :].rearrange("p v q -> p (v q)"), in_=lp[:])
+            nc.tensor.matmul(out=fps[:, kind, :], lhsT=ffv[:, kind, :], rhs=ident_b[:, 0:4], start=True, stop=True)
+        nc.scalar.copy(out=xx[:, 0:8], in_=fps[:].rearrange("p k f -> p (k f)"))
+        for kind in range(2):
             lq = ps_tile([P, 256], F32, "bk")
             nc.tensor.matmul(
-                out=lq[:], lhsT=ffm[:, 0, kind, :], rhs=sel[:, 4:6, :].rearrange("p v q -> p (v q)"), start=True, stop=False
+                out=lq[:], lhsT=ffm[:, 0, kind, :], rhs=sel[:, 0:2, :].rearrange("p v q -> p (v q)"), start=True, stop=False
             )
             nc.tensor.matmul(
-                out=lq[:], lhsT=ffm[:, 1, kind, :], rhs=sel[:, 6:8, :].rearrange("p v q -> p (v q)"), start=False, stop=True
+                out=lq[:], lhsT=ffm[:, 1, kind, :], rhs=sel[:, 2:4, :].rearrange("p v q -> p (v q)"), start=False, stop=True
             )
-            nc.scalar.copy(out=lsb[:, kind, 4:6, :].rearrange("p v q -> p (v q)"), in_=lq[:])
+            nc.scalar.copy(out=lsb[:, kind, :, :].rearrange("p v q -> p (v q)"), in_=lq[:])
 
         rd = {}
 
@@ -363,7 +360,6 @@ def tile_wanselfattention_pa_kernel(
 
         make_rd(0)
 
-        nc.scalar.copy(out=xx[:, 0:8].rearrange("p (k f) -> p k f", k=2), in_=lsb[:, :, 0:4, 0])
         scr = outs[1][TOK - 16 : TOK, :].rearrange("r c -> (r c)")
         NROW = 16 * NH * W1
 
@@ -414,15 +410,15 @@ def tile_wanselfattention_pa_kernel(
                 )
                 defer(
                     1,
-                    lambda: nc.scalar.copy(
-                        out=dst[:, kind, 6 * half : 6 * (half + 1), :].rearrange("p h d -> p (h d)"), in_=tb[:, 0:n]
+                    lambda: evac(
+                        "v" if pj == 1 else "s", dst[:, kind, 6 * half : 6 * (half + 1), :].rearrange("p h d -> p (h d)"), tb[:, 0:n]
                     ),
                 )
 
             return [lambda kind=kind, half=half: job(kind, half) for kind in range(2) for half in range(2)]
-        fill.extend(table_jobs(0, 1, 4, ("t23", 0, 0)))
+        fill.extend(table_jobs(0, 1, 0, ("t23", 0, 0)))
         fill.extend(row_jobs(0))
-        fill.extend(table_jobs(0, 1, 5, ("t23", 0, 1)))
+        fill.extend(table_jobs(0, 1, 1, ("t23", 0, 1)))
         fill.extend(x_jobs(1))
         fill.extend(x_jobs(2))
         fill.append(lambda: defer(3, lambda: load_tab1(0)))
@@ -430,8 +426,8 @@ def tile_wanselfattention_pa_kernel(
         fill.append(lambda: make_rd(1))
         fill.extend(row_jobs(1))
         fill.extend(x_jobs(3))
-        fill.extend(table_jobs(1, 1, 4, ("t23", 1, 0)))
-        fill.extend(table_jobs(1, 1, 5, ("t23", 1, 1)))
+        fill.extend(table_jobs(1, 1, 0, ("t23", 1, 0)))
+        fill.extend(table_jobs(1, 1, 1, ("t23", 1, 1)))
 
         for k in range(1, 7):
             for j in range(3):
@@ -442,7 +438,7 @@ def tile_wanselfattention_pa_kernel(
                     LD("q", k + 3)
                     LD("x", k + 1)
                 if k >= 1:
-                    start_prep("q", k - 1, j, "bk", "s")
+                    start_prep("q", k - 1, j, "bk", "v" if k == 6 else "s")
                     if j == 2:
                         defer(3, lambda a=k - 1: start_mx(0, a, ("s", "s")))
                 do_fill(HEAD_FILL)

@@ -61,16 +61,20 @@ def tile_wanselfattention_pa_kernel(
             else:
                 nc.vector.tensor_copy(out=out, in_=in_)
 
+        sc_rows = const.tile([P, P], F32, name="sc_rows")
+        nc.vector.memset(sc_rows[:], 0.0)
+        nc.sync.dma_start(out=sc_rows[0:NH, :], in_=Wq_scale.rearrange("o (r n) -> (o r) n", n=P))
         scale_bc = const.tile([P, DIM], F32, name="scale_bc")
-        nc.sync.dma_start(out=scale_bc[:], in_=Wq_scale.rearrange("o k -> (o k)").partition_broadcast(P))
         vecs = const.tile([P, P], BF16, name="vecs")
         nc.vector.memset(vecs[:], 0.0)
-        for i, vec in enumerate((bq, bk, gq, gk)):
-            nc.scalar.dma_start(out=vecs[NH * i : NH * (i + 1), :], in_=vec.rearrange("(h d) -> h d", d=P))
         fc = const.tile([P, 2, 64], BF16, name="fc")
         nc.vector.memset(fc[:], 0.0)
-        nc.scalar.dma_start(out=fc[0:16, 0, :], in_=freqs_cos[0:16, :])
-        nc.scalar.dma_start(out=fc[0:16, 1, :], in_=freqs_sin[0:16, :])
+
+        def small_loads():
+            for i, vec in enumerate((bq, bk, gq, gk)):
+                nc.sync.dma_start(out=vecs[NH * i : NH * (i + 1), :], in_=vec.rearrange("(h d) -> h d", d=P))
+            nc.sync.dma_start(out=fc[0:16, 0, :], in_=freqs_cos[0:16, :])
+            nc.sync.dma_start(out=fc[0:16, 1, :], in_=freqs_sin[0:16, :])
 
         one = const.tile([P, 1], F32, name="one")
         nc.vector.memset(one[:], 1.0)
@@ -119,9 +123,14 @@ def tile_wanselfattention_pa_kernel(
             if i == 0:
                 wq_val = work.tile([P, 2, DIM], BF16, name="wq_val", tag="wq_val", bufs=2)
                 st_rows[("q", a)] = wq_val
-            nc.vector.tensor_tensor(
-                out=st_rows[("q", a)][:, i, :], in0=st_rows[("qb", a)][:, i, :].bitcast(FP8), in1=scale_bc[:], op=ALU.mult
-            )
+            step = 512 if (a == 0 and i == 0) else DIM
+            for c in range(0, DIM, step):
+                nc.vector.tensor_tensor(
+                    out=st_rows[("q", a)][:, i, c : c + step],
+                    in0=st_rows[("qb", a)][:, i, c : c + step].bitcast(FP8),
+                    in1=scale_bc[:, c : c + step],
+                    op=ALU.mult,
+                )
 
         def TR(s, a, g, tag):
             words = st_rows[(s, a)][:].rearrange("p i k -> p (i k)").bitcast(F32)
@@ -157,6 +166,7 @@ def tile_wanselfattention_pa_kernel(
 
         LD("q", 0)
         LD("x", 0)
+        small_loads()
         for a in range(1, 3):
             LD("q", a)
         pending = []
@@ -305,6 +315,16 @@ def tile_wanselfattention_pa_kernel(
                 out=sel[:, 2 + hh, :].rearrange("p (a b) -> p a b", b=16),
                 in_=ident_b[:, 0:16].unsqueeze(1).to_broadcast([P, 8, 16]),
             )
+
+        sc_ps = ps_tile([P, P], F32, "acc")
+        nc.tensor.transpose(sc_ps[:], sc_rows[:], ident_f[:])
+        sc_cols = const.tile([P, NH], F32, name="sc_cols")
+        nc.scalar.copy(out=sc_cols[:], in_=sc_ps[:, 0:NH])
+        for j in range(3):
+            sps = ps_tile([P, 4, P], F32, "acc")
+            for r in range(4):
+                nc.tensor.transpose(sps[:, r, :], sc_cols[:, 4 * j + r : 4 * j + r + 1].to_broadcast([P, P]), ident_f[:])
+            nc.scalar.copy(out=scale_bc[:, 512 * j : 512 * (j + 1)], in_=sps[:].rearrange("p r n -> p (r n)"))
 
         for j in range(3):
             tick()

@@ -23,10 +23,12 @@ W1 = 44
 W23 = 84
 FLOPS = 2 * TOK * DIM * 2 * DIM
 PS_BUFS = {"acc": 3, "bk": 5}
-HEAD_FILL = 1
+DOUBLE = ((2, 1), (3, 1), (4, 1))
 SLOT_FILL = 1
 TE_V_FROM = 6
 TE_V_J = ()
+RD_EARLY = (0, 1)
+SC_ENG = ("s", "s", "s")
 EX_ENG = ("v", "s", "s")
 
 
@@ -61,17 +63,19 @@ def tile_wanselfattention_pa_kernel(
             else:
                 nc.vector.tensor_copy(out=out, in_=in_)
 
-        sc_rows = const.tile([P, P], F32, name="sc_rows")
-        nc.vector.memset(sc_rows[:], 0.0)
-        nc.sync.dma_start(out=sc_rows[0:NH, :], in_=Wq_scale.rearrange("o (r n) -> (o r) n", n=P))
+        scl = const.tile([P, PASSES, 4], F32, name="scl")
+        nc.sync.dma_start(out=scl[:], in_=Wq_scale.rearrange("o (g p t) -> p (o g) t", p=P, t=4))
         scale_bc = const.tile([P, DIM], F32, name="scale_bc")
+        gq_rows = const.tile([P, P], BF16, name="gq_rows")
+        nc.vector.memset(gq_rows[:], 0.0)
+        nc.sync.dma_start(out=gq_rows[0:NH, :], in_=gq.rearrange("(h d) -> h d", d=P))
         vecs = const.tile([P, P], BF16, name="vecs")
         nc.vector.memset(vecs[:], 0.0)
         fc = const.tile([P, 2, 64], BF16, name="fc")
         nc.vector.memset(fc[:], 0.0)
 
         def small_loads():
-            for i, vec in enumerate((bq, bk, gq, gk)):
+            for i, vec in enumerate((bq, bk, gk)):
                 nc.sync.dma_start(out=vecs[NH * i : NH * (i + 1), :], in_=vec.rearrange("(h d) -> h d", d=P))
             nc.sync.dma_start(out=fc[0:16, 0, :], in_=freqs_cos[0:16, :])
             nc.sync.dma_start(out=fc[0:16, 1, :], in_=freqs_sin[0:16, :])
@@ -316,15 +320,41 @@ def tile_wanselfattention_pa_kernel(
                 in_=ident_b[:, 0:16].unsqueeze(1).to_broadcast([P, 8, 16]),
             )
 
-        sc_ps = ps_tile([P, P], F32, "acc")
-        nc.tensor.transpose(sc_ps[:], sc_rows[:], ident_f[:])
-        sc_cols = const.tile([P, NH], F32, name="sc_cols")
-        nc.scalar.copy(out=sc_cols[:], in_=sc_ps[:, 0:NH])
-        for j in range(3):
+        gain_cols = {}
+
+        def turn_gains():
+            gps = ps_tile([P, P], BF16, "bk")
+            nc.tensor.transpose(gps[:], gq_rows[:], ident_b[:])
+            gq_cols = const.tile([P, NH], F32, name="gq_cols")
+            nc.scalar.copy(out=gq_cols[:], in_=gps[:, 0:NH])
+            gain_cols[0] = gq_cols[:]
+
+        rd = {0: [], 1: []}
+
+        def make_rd(pj, part):
+            off, w = ((0, W1), (W1, W23))[part]
+            r_t = const.tile([P, NH, w], BF16, name="rd%d%d" % (pj, part))
+            nc.vector.tensor_tensor(
+                out=r_t[:],
+                in0=ident_b[:, off : off + w].unsqueeze(1).to_broadcast([P, NH, w]),
+                in1=gain_cols[pj].unsqueeze(2).to_broadcast([P, NH, w]),
+                op=ALU.mult,
+            )
+            rd[pj].append(r_t)
+
+        turn_gains()
+        for part in RD_EARLY:
+            make_rd(0, part)
+
+        for g in range(PASSES):
             sps = ps_tile([P, 4, P], F32, "acc")
-            for r in range(4):
-                nc.tensor.transpose(sps[:, r, :], sc_cols[:, 4 * j + r : 4 * j + r + 1].to_broadcast([P, P]), ident_f[:])
-            nc.scalar.copy(out=scale_bc[:, 512 * j : 512 * (j + 1)], in_=sps[:].rearrange("p r n -> p (r n)"))
+            for t in range(4):
+                nc.tensor.transpose(sps[:, t, :], scl[:, g, t : t + 1].to_broadcast([P, P]), ident_f[:])
+            evac(
+                SC_ENG[g],
+                scale_bc[:, 512 * g : 512 * (g + 1)].rearrange("p (n t) -> p n t", t=4),
+                sps[:].rearrange("p t n -> p n t"),
+            )
 
         for j in range(3):
             tick()
@@ -337,8 +367,9 @@ def tile_wanselfattention_pa_kernel(
 
         vps = ps_tile([P, P], BF16, "acc")
         nc.tensor.transpose(vps[:], vecs[:], ident_b[:])
-        cols = const.tile([P, 48], F32, name="cols")
-        nc.scalar.copy(out=cols[:], in_=vps[:, 0:48])
+        cols = const.tile([P, 36], F32, name="cols")
+        nc.scalar.copy(out=cols[:], in_=vps[:, 0:36])
+        gain_cols[1] = cols[:, 24:36]
 
         ff = const.tile([P, 2, 64, 2], BF16, name="ff")
         nc.scalar.copy(out=ff[:, 0, :, :], in_=fc[:, 0, :].unsqueeze(2).to_broadcast([P, 64, 2]))
@@ -363,22 +394,8 @@ def tile_wanselfattention_pa_kernel(
             )
             nc.scalar.copy(out=lsb[:, kind, :, :].rearrange("p v q -> p (v q)"), in_=lq[:])
 
-        rd = {}
-
-        def make_rd(pj):
-            parts = []
-            for part, (off, w) in enumerate(((0, W1), (W1, W23))):
-                r_t = const.tile([P, NH, w], BF16, name="rd%d%d" % (pj, part))
-                nc.vector.tensor_tensor(
-                    out=r_t[:],
-                    in0=ident_b[:, off : off + w].unsqueeze(1).to_broadcast([P, NH, w]),
-                    in1=cols[:, 24 + NH * pj : 24 + NH * (pj + 1)].unsqueeze(2).to_broadcast([P, NH, w]),
-                    op=ALU.mult,
-                )
-                parts.append(r_t)
-            rd[pj] = parts
-
-        make_rd(0)
+        for part in range(len(RD_EARLY), 2):
+            make_rd(0, part)
 
         scr = outs[1][TOK - 16 : TOK, :].rearrange("r c -> (r c)")
         NROW = 16 * NH * W1
@@ -441,11 +458,11 @@ def tile_wanselfattention_pa_kernel(
         fill.extend(table_jobs(0, 1, 1, ("t23", 0, 1)))
         fill.extend(x_jobs(1))
         fill.extend(x_jobs(2))
+        fill.extend(x_jobs(3))
         fill.append(lambda: defer(3, lambda: load_tab1(0)))
         fill.append(lambda: defer(3, lambda: load_tab1(1)))
-        fill.append(lambda: make_rd(1))
+        fill.append(lambda: (make_rd(1, 0), make_rd(1, 1)))
         fill.extend(row_jobs(1))
-        fill.extend(x_jobs(3))
         fill.extend(table_jobs(1, 1, 0, ("t23", 1, 0)))
         fill.extend(table_jobs(1, 1, 1, ("t23", 1, 1)))
 
@@ -461,7 +478,7 @@ def tile_wanselfattention_pa_kernel(
                     start_prep("q", k - 1, j, "bk", "v" if k == 6 else "s")
                     if j == 2:
                         defer(3, lambda a=k - 1: start_mx(0, a, ("s", "s")))
-                do_fill(HEAD_FILL)
+                do_fill(2 if (k, j) in DOUBLE else 1)
         for a in range(2):
             LD("k", a)
         fill_tag[0] = "acc"

from contextlib import ExitStack

import concourse.mybir as mybir
from concourse.masks import make_identity

F32 = mybir.dt.float32
BF16 = mybir.dt.bfloat16
U32 = mybir.dt.uint32
U8 = mybir.dt.uint8
FP8 = mybir.dt.float8_e4m3fn
FP8X4 = mybir.dt.float8_e4m3fn_x4
ALU = mybir.AluOpType
ACT = mybir.ActivationFunctionType

P = 128
TOK = 1024
DIM = 1536
NH = 12
PASSES = 3
BLK = 256
EPS = 1e-6
W1 = 44
W23 = 84
FLOPS = 2 * TOK * DIM * 2 * DIM
PS_BUFS = {"acc": 3, "bk": 5}
DOUBLE = ((2, 1), (3, 1), (4, 1))
SLOT_FILL = 1
TE_V_FROM = 6
TE_V_J = ()
RD_EARLY = (0, 1)
SC_ENG = ("s", "s", "s")
EX_ENG = ("v", "s", "s")


def tile_wanselfattention_pa_kernel(
    tc, x, Wq_bytes, Wq_scale, bq, Wk, bk, gq, gk, freqs_cos, freqs_sin, out_0, out_1
):
    nc = tc.nc
    outs = (out_0.rearrange("s h d -> s (h d)"), out_1.rearrange("s h d -> s (h d)"))

    with ExitStack() as ctx:
        const = ctx.enter_context(tc.tile_pool(name="const", bufs=1))
        work = ctx.enter_context(tc.tile_pool(name="work", bufs=2))
        psum = ctx.enter_context(tc.psum_pool(name="psum", bufs=3))

        ctx.enter_context(tc.manual_schedule())

        def ps_tile(shape, dtype, tag):
            return psum.tile(shape, dtype, name="ps_" + tag, tag=tag, bufs=PS_BUFS[tag])

        early_count = [0]

        def early_tag():
            early_count[0] += 1
            return "acc" if early_count[0] % 8 < 3 else "bk"

        def early_tags():
            return (early_tag(), early_tag(), early_tag())

        def evac(eng, out, in_):
            if eng == "s":
                nc.scalar.copy(out=out, in_=in_)
            else:
                nc.vector.tensor_copy(out=out, in_=in_)

        scl = const.tile([P, PASSES, 4], F32, name="scl")
        nc.sync.dma_start(out=scl[:], in_=Wq_scale.rearrange("o (g p t) -> p (o g) t", p=P, t=4))
        scale_bc = const.tile([P, DIM], F32, name="scale_bc")
        gq_rows = const.tile([P, P], BF16, name="gq_rows")
        nc.vector.memset(gq_rows[:], 0.0)
        nc.sync.dma_start(out=gq_rows[0:NH, :], in_=gq.rearrange("(h d) -> h d", d=P))
        vecs = const.tile([P, P], BF16, name="vecs")
        nc.vector.memset(vecs[:], 0.0)
        fc = const.tile([P, 2, 64], BF16, name="fc")
        nc.vector.memset(fc[:], 0.0)

        def small_loads():
            for i, vec in enumerate((bq, bk, gk)):
                nc.sync.dma_start(out=vecs[NH * i : NH * (i + 1), :], in_=vec.rearrange("(h d) -> h d", d=P))
            nc.sync.dma_start(out=fc[0:16, 0, :], in_=freqs_cos[0:16, :])
            nc.sync.dma_start(out=fc[0:16, 1, :], in_=freqs_sin[0:16, :])

        one = const.tile([P, 1], F32, name="one")
        nc.vector.memset(one[:], 1.0)
        ffm = const.tile([P, 2, 2, P], BF16, name="ffm")
        nc.vector.memset(ffm[:], 0.0)
        xx = const.tile([P, P], BF16, name="xx")
        nc.vector.memset(xx[:], 0.0)
        warm = const.tile([P, 1], F32, name="warm")
        nc.scalar.activation(out=warm[:], in_=one[:], func=ACT.Abs_reciprocal_sqrt)

        ident_f = const.tile([P, P], F32, name="ident_f")
        make_identity(nc, ident_f[:])
        ident_b = const.tile([P, P], BF16, name="ident_b")
        make_identity(nc, ident_b[:])

        cx = const.tile([P, TOK // BLK, PASSES, BLK], U32, name="cx", align_bytes=64)
        sx = const.tile([P, TOK // BLK, PASSES, BLK], U8, name="sx", align_bytes=64)
        cw = []
        sw = []
        for pj in range(2):
            cw_t = const.tile([P, DIM // BLK, PASSES, BLK], U32, name="cw%d" % pj, align_bytes=64)
            sw_t = const.tile([P, DIM // BLK, PASSES, BLK], U8, name="sw%d" % pj, align_bytes=64)
            cw.append(cw_t)
            sw.append(sw_t)

        st_rows = {}
        st_tp = {}
        st_gr = {}
        SRC = {"x": (x, cx, sx), "q": (None, cw[0], sw[0]), "k": (Wk, cw[1], sw[1])}

        def LD(s, a):
            if s == "q":
                wq_bytes = work.tile([P, 2, DIM], U8, name="wq_bytes", tag="wq_bytes", bufs=3)
                nc.sync.dma_start(
                    out=wq_bytes[:], in_=Wq_bytes[BLK * a : BLK * (a + 1), :].rearrange("(i p) k -> p i k", p=P)
                )
                st_rows[("qb", a)] = wq_bytes
            else:
                t = work.tile([P, 2, DIM], BF16, name="rows", tag="rows", bufs=4)
                nc.sync.dma_start(
                    out=t[:], in_=SRC[s][0][BLK * a : BLK * (a + 1), :].rearrange("(i p) k -> p i k", p=P)
                )
                st_rows[(s, a)] = t

        def PRD(a, i):
            if i == 0:
                wq_val = work.tile([P, 2, DIM], BF16, name="wq_val", tag="wq_val", bufs=2)
                st_rows[("q", a)] = wq_val
            step = 512 if (a == 0 and i == 0) else DIM
            for c in range(0, DIM, step):
                nc.vector.tensor_tensor(
                    out=st_rows[("q", a)][:, i, c : c + step],
                    in0=st_rows[("qb", a)][:, i, c : c + step].bitcast(FP8),
                    in1=scale_bc[:, c : c + step],
                    op=ALU.mult,
                )

        def TR(s, a, g, tag):
            words = st_rows[(s, a)][:].rearrange("p i k -> p (i k)").bitcast(F32)
            tp = ps_tile([P, 2, 2, P], F32, tag)
            for i in range(2):
                for u in range(2):
                    base = i * (DIM // 2) + 256 * g + u
                    nc.tensor.transpose(tp[:, i, u, :], words[:, base : base - u + 256 : 2], ident_f[:])
            st_tp[(s, a, g)] = tp

        def EX(s, a, g, eng):
            if g == 0:
                gr01 = work.tile([P, 2, BLK * 4], BF16, name="gr01", tag="gr01", bufs=2, align_bytes=64)
                st_gr[(s, a, 0)] = gr01
            if g == 2:
                gr2 = work.tile([P, 1, BLK * 4], BF16, name="gr2", tag="gr2", bufs=2, align_bytes=64)
                st_gr[(s, a, 2)] = gr2
            evac(
                eng,
                st_gr[(s, a, 2 * (g // 2))][:, g % 2, :].bitcast(F32).rearrange("p (i r u) -> p i r u", i=2, u=2),
                st_tp[(s, a, g)][:].rearrange("p i u r -> p i r u"),
            )

        def QZ(s, a, g):
            if g == 0:
                return
            g0 = 2 * (g // 2)
            nc.vector.quantize_mx(
                out=SRC[s][1][:, a, g0 : g + 1, :].rearrange("p g c -> p (g c)").bitcast(FP8X4),
                scales=SRC[s][2][:, a, g0 : g + 1, :].rearrange("p g c -> p (g c)"),
                in_=st_gr[(s, a, g0)][:].rearrange("p g c -> p (g c)"),
            )

        LD("q", 0)
        LD("x", 0)
        small_loads()
        for a in range(1, 3):
            LD("q", a)
        pending = []
        clock = [0]

        def defer(delay, fn):
            pending.append((clock[0] + delay, fn))

        def tick():
            clock[0] += 1
            due = [p for p in pending if p[0] <= clock[0]]
            rest = [p for p in pending if p[0] > clock[0]]
            pending.clear()
            pending.extend(rest)
            for p in due:
                p[1]()


        blks = [(0, 0), (0, 1), (0, 2), (0, 3), (1, 0), (1, 1), (1, 2), (1, 3)]
        tts = {}
        st_acc = {}
        st_bk = {}
        st_ss = {}
        st_rstd = {}
        st_uv = {}

        def MXB(n, mp):
            pj, blk = blks[n]
            acc = ps_tile([P, 2, BLK], F32, "acc")
            for mi in range(2):
                m = 2 * mp + mi
                for g in range(PASSES):
                    nc.tensor.matmul_mx(
                        out=acc[:, mi, :],
                        lhsT=cw[pj][:, mp, g, P * mi : P * (mi + 1)].bitcast(FP8X4),
                        lhsT_scale=sw[pj][:, mp, g, P * mi : P * (mi + 1)],
                        rhs=cx[:, blk, g, :].bitcast(FP8X4),
                        rhs_scale=sx[:, blk, g, :],
                        start=(g == 0),
                        stop=(g == PASSES - 1),
                    )
            st_acc[(n, mp)] = acc

        def TE(n, mp, engs):
            pj = blks[n][0]
            for mi in range(2):
                m = 2 * mp + mi
                t = work.tile([P, BLK], F32, name="tT", tag="tT", bufs=26)
                bias = cols[:, NH * pj + m : NH * pj + m + 1]
                if engs[mi] == "s":
                    nc.scalar.activation(out=t[:], in_=st_acc[(n, mp)][:, mi, :], func=ACT.Identity, bias=bias)
                else:
                    nc.vector.tensor_scalar(
                        out=t[:], in0=st_acc[(n, mp)][:, mi, :], scalar1=bias, scalar2=None, op0=ALU.add
                    )
                tts[(n, m)] = t

        def BT(s, b3):
            bkt = ps_tile([P, 4, P], F32, "bk")
            i = s % 2
            for q in range(4):
                nc.tensor.transpose(bkt[:, q, :], tts[(s // 2, 4 * b3 + q)][:, P * i : P * (i + 1)], ident_f[:])
            st_bk[(s, b3)] = bkt

        def SQ(s, b3):
            if b3 == 0:
                ss_t = work.tile([P, 8], F32, name="ss", tag="ss", bufs=4)
                st_ss[s] = ss_t
            junk = work.tile([P, 512], BF16, name="junk", tag="junk", bufs=2)
            nc.scalar.activation(
                out=junk[:],
                in_=st_bk[(s, b3)][:].rearrange("p q d -> p (q d)"),
                func=ACT.Square,
                accum_out=st_ss[s][:, b3 : b3 + 1],
            )

        def RS(s):
            ss_t = st_ss[s]
            nc.scalar.activation(out=ss_t[:, 4:7], in_=ss_t[:, 0:3], func=ACT.Identity, accum_out=ss_t[:, 3:4])
            nc.scalar.activation(
                out=ss_t[:, 7:8], in_=ss_t[:, 3:4], func=ACT.Abs_reciprocal_sqrt, scale=1.0 / DIM, bias=EPS
            )

        def RC(s):
            st_rstd[s] = st_ss[s][:, 7:8]

        def UV(s, b3):
            n = s // 2
            parts = ((0, W1, tabs[("t1", n)]), (W1, W23, tabs[("t23", blks[n][0], s % 2)]))
            for kind, tag in enumerate(("u", "v")):
                pr_t = work.tile([P, 4, P], F32, name=tag, tag=tag, bufs=3)
                for off, w, tab in parts:
                    nc.vector.scalar_tensor_tensor(
                        out=pr_t[:, :, off : off + w],
                        in0=st_bk[(s, b3)][:, :, off : off + w],
                        scalar=st_rstd[s],
                        in1=tab[:, kind, 4 * b3 : 4 * (b3 + 1), :],
                        op0=ALU.mult,
                        op1=ALU.mult,
                    )
                st_uv[(s, b3, kind)] = pr_t

        def MG(s, b3):
            o_t = work.tile([P, 512], F32, name="o", tag="o", bufs=6)
            eng = nc.vector if (s == 15 and b3 >= 2) else nc.gpsimd
            eng.tensor_tensor(
                out=o_t[:].rearrange("p (c e) -> p c e", e=2),
                in0=st_uv[(s, b3, 0)][:].rearrange("p q (c e) -> p (q c) e", e=2),
                in1=st_uv[(s, b3, 1)][:].rearrange("p q (c e) -> p (q c) e", e=2)[:, :, ::-1],
                op=ALU.add,
            )
            pj, blk = blks[s // 2]
            row0 = P * (2 * blk + s % 2)
            nc.sync.dma_start(out=outs[pj][row0 : row0 + P, 512 * b3 : 512 * (b3 + 1)], in_=o_t[:])

        def start_prep(src, a, g, tag, eng):
            TR(src, a, g, tag)
            defer(1, lambda: EX(src, a, g, eng))
            defer(2, lambda: QZ(src, a, g))

        def start_mx(n, mp, engs):
            MXB(n, mp)
            defer(1, lambda: TE(n, mp, engs))

        fill = []
        fill_tag = ["bk"]
        fill_pos = [0]

        def do_fill(count):
            for r in range(count):
                if fill_pos[0] < len(fill):
                    fill[fill_pos[0]]()
                    fill_pos[0] += 1

        def x_jobs(a):
            return [lambda g=g: start_prep("x", a, g, fill_tag[0], "s") for g in range(PASSES)]


        sel = const.tile([P, 4, P], BF16, name="sel")
        for hh in range(2):
            nc.vector.tensor_copy(
                out=sel[:, hh, :].rearrange("p (a b) -> p a b", b=16),
                in_=ident_b[:, 8 * hh : 8 * hh + 8].unsqueeze(2).to_broadcast([P, 8, 16]),
            )
            nc.vector.tensor_copy(
                out=sel[:, 2 + hh, :].rearrange("p (a b) -> p a b", b=16),
                in_=ident_b[:, 0:16].unsqueeze(1).to_broadcast([P, 8, 16]),
            )

        gain_cols = {}

        def turn_gains():
            gps = ps_tile([P, P], BF16, "bk")
            nc.tensor.transpose(gps[:], gq_rows[:], ident_b[:])
            gq_cols = const.tile([P, NH], F32, name="gq_cols")
            nc.scalar.copy(out=gq_cols[:], in_=gps[:, 0:NH])
            gain_cols[0] = gq_cols[:]

        rd = {0: [], 1: []}

        def make_rd(pj, part):
            off, w = ((0, W1), (W1, W23))[part]
            r_t = const.tile([P, NH, w], BF16, name="rd%d%d" % (pj, part))
            nc.vector.tensor_tensor(
                out=r_t[:],
                in0=ident_b[:, off : off + w].unsqueeze(1).to_broadcast([P, NH, w]),
                in1=gain_cols[pj].unsqueeze(2).to_broadcast([P, NH, w]),
                op=ALU.mult,
            )
            rd[pj].append(r_t)

        turn_gains()
        for part in RD_EARLY:
            make_rd(0, part)

        for g in range(PASSES):
            sps = ps_tile([P, 4, P], F32, "acc")
            for t in range(4):
                nc.tensor.transpose(sps[:, t, :], scl[:, g, t : t + 1].to_broadcast([P, P]), ident_f[:])
            evac(
                SC_ENG[g],
                scale_bc[:, 512 * g : 512 * (g + 1)].rearrange("p (n t) -> p n t", t=4),
                sps[:].rearrange("p t n -> p n t"),
            )

        for j in range(3):
            tick()
            if j < 2:
                PRD(0, j)
            else:
                LD("q", 3)
                LD("x", 1)
            start_prep("x", 0, j, "bk", "s")

        vps = ps_tile([P, P], BF16, "acc")
        nc.tensor.transpose(vps[:], vecs[:], ident_b[:])
        cols = const.tile([P, 36], F32, name="cols")
        nc.scalar.copy(out=cols[:], in_=vps[:, 0:36])
        gain_cols[1] = cols[:, 24:36]

        ff = const.tile([P, 2, 64, 2], BF16, name="ff")
        nc.scalar.copy(out=ff[:, 0, :, :], in_=fc[:, 0, :].unsqueeze(2).to_broadcast([P, 64, 2]))
        nc.scalar.copy(out=ff[:, 1, :, 0], in_=fc[:, 1, :])
        nc.scalar.mul(out=ff[:, 1, :, 1], in_=fc[:, 1, :], mul=-1.0)
        ffv = ff[:].rearrange("p k c e -> p k (c e)")
        nc.scalar.copy(out=ffm[:, 0, :, 44:86], in_=ffv[:, :, 44:86])
        nc.scalar.copy(out=ffm[:, 1, :, 86:128], in_=ffv[:, :, 86:128])

        lsb = const.tile([P, 2, 2, P], BF16, name="lsb")
        fps = ps_tile([P, 2, 4], F32, "bk")
        for kind in range(2):
            nc.tensor.matmul(out=fps[:, kind, :], lhsT=ffv[:, kind, :], rhs=ident_b[:, 0:4], start=True, stop=True)
        nc.scalar.copy(out=xx[:, 0:8], in_=fps[:].rearrange("p k f -> p (k f)"))
        for kind in range(2):
            lq = ps_tile([P, 256], F32, "bk")
            nc.tensor.matmul(
                out=lq[:], lhsT=ffm[:, 0, kind, :], rhs=sel[:, 0:2, :].rearrange("p v q -> p (v q)"), start=True, stop=False
            )
            nc.tensor.matmul(
                out=lq[:], lhsT=ffm[:, 1, kind, :], rhs=sel[:, 2:4, :].rearrange("p v q -> p (v q)"), start=False, stop=True
            )
            nc.scalar.copy(out=lsb[:, kind, :, :].rearrange("p v q -> p (v q)"), in_=lq[:])

        for part in range(len(RD_EARLY), 2):
            make_rd(0, part)

        scr = outs[1][TOK - 16 : TOK, :].rearrange("r c -> (r c)")
        NROW = 16 * NH * W1

        def row_jobs(pj):
            r1 = const.tile([P, NH * W1], F32, name="r1_%d" % pj)
            n = 6 * W1

            def job(half):
                flat = rd[pj][0][:].rearrange("p h d -> p (h d)")
                tb = ps_tile([P, 512], F32, fill_tag[0])
                nc.tensor.matmul(out=tb[:, 0:n], lhsT=xx[:], rhs=flat[:, n * half : n * (half + 1)], start=True, stop=True)
                defer(1, lambda: nc.scalar.copy(out=r1[:, n * half : n * (half + 1)], in_=tb[:, 0:n]))

            def store():
                nc.sync.dma_start(
                    out=scr[NROW * pj : NROW * (pj + 1)].rearrange("(r n) -> r n", n=NH * W1), in_=r1[0:16, :]
                )

            return [lambda: job(0), lambda: job(1), lambda: defer(2, store)]

        def load_tab1(n):
            pj, f = blks[n]
            t = work.tile([P, 2, NH, W1], F32, name="tab1", tag="tab1", bufs=3)
            rows = scr[NROW * pj : NROW * pj + 8 * NH * W1].rearrange("(k f n) -> f k n", k=2, f=4)
            nc.sync.dma_start(out=t[:].rearrange("p k h d -> p k (h d)"), in_=rows[f].partition_broadcast(P))
            tabs[("t1", n)] = t

        tabs = {}

        def table_jobs(pj, part, var, key):
            w = (W1, W23)[part]
            n = 6 * w
            if part == 0:
                dst = work.tile([P, 2, NH, W1], F32, name="tab1", tag="tab1", bufs=3)
            else:
                dst = const.tile([P, 2, NH, W23], F32, name="tab23_%d%d" % (pj, var))
            tabs[key] = dst

            def job(kind, half):
                flat = rd[pj][part][:].rearrange("p h d -> p (h d)")
                tb = ps_tile([P, 512], F32, fill_tag[0])
                nc.tensor.matmul(
                    out=tb[:, 0:n],
                    lhsT=lsb[:, kind, var, :],
                    rhs=flat[:, n * half : n * (half + 1)],
                    start=True,
                    stop=True,
                )
                defer(
                    1,
                    lambda: evac(
                        "v" if pj == 1 else "s", dst[:, kind, 6 * half : 6 * (half + 1), :].rearrange("p h d -> p (h d)"), tb[:, 0:n]
                    ),
                )

            return [lambda kind=kind, half=half: job(kind, half) for kind in range(2) for half in range(2)]
        fill.extend(table_jobs(0, 1, 0, ("t23", 0, 0)))
        fill.extend(row_jobs(0))
        fill.extend(table_jobs(0, 1, 1, ("t23", 0, 1)))
        fill.extend(x_jobs(1))
        fill.extend(x_jobs(2))
        fill.extend(x_jobs(3))
        fill.append(lambda: defer(3, lambda: load_tab1(0)))
        fill.append(lambda: defer(3, lambda: load_tab1(1)))
        fill.append(lambda: (make_rd(1, 0), make_rd(1, 1)))
        fill.extend(row_jobs(1))
        fill.extend(table_jobs(1, 1, 0, ("t23", 1, 0)))
        fill.extend(table_jobs(1, 1, 1, ("t23", 1, 1)))

        for k in range(1, 7):
            for j in range(3):
                tick()
                if k < 6 and j < 2:
                    PRD(k, j)
                if j == 2 and k < 3:
                    LD("q", k + 3)
                    LD("x", k + 1)
                if k >= 1:
                    start_prep("q", k - 1, j, "bk", "v" if k == 6 else "s")
                    if j == 2:
                        defer(3, lambda a=k - 1: start_mx(0, a, ("s", "s")))
                do_fill(2 if (k, j) in DOUBLE else 1)
        for a in range(2):
            LD("k", a)
        fill_tag[0] = "acc"

        def front(nx, j):
            if j == 0:
                BT(nx, 0)
                BT(nx, 1)
                SQ(nx, 0)
                SQ(nx, 1)
            elif j == 1:
                BT(nx, 2)
                SQ(nx, 2)
                RS(nx)
            else:
                RC(nx)

        tick()
        front(0, 0)
        start_mx(1, 0, ("s", "s"))
        do_fill(1)
        tick()
        start_mx(1, 1, ("s", "s"))
        do_fill(1)
        tick()
        do_fill(1)
        tick()
        front(0, 1)
        start_mx(1, 2, ("s", "s"))
        do_fill(1)
        tick()
        front(0, 2)

        for s in range(16):
            nb = (s + 1) // 2 + 1
            mps = [3 * ((s + 1) % 2) + r for r in range(3)] if nb < 8 else []
            for j in range(3):
                tick()
                if s + 1 < 16 and j < 2:
                    front(s + 1, j)
                UV(s, j)
                MG(s, j)
                if mps:
                    te = ("s", "v") if (s >= TE_V_FROM and j in TE_V_J) else ("s", "s")
                    start_mx(nb, mps[j], te)
                if s <= 5:
                    start_prep("k", s, j, "acc", EX_ENG[j])
                    if j == 2 and s + 2 < 6:
                        LD("k", s + 2)
                if s + 1 < 16 and j == 2:
                    front(s + 1, 2)
                if j == 0 and s % 2 == 0 and s // 2 + 2 < 8:
                    n2 = s // 2 + 2
                    load_tab1(n2)
                do_fill(SLOT_FILL)
        for r in range(4):
            tick()
